import numpy as np
import ml_dtypes

BF16 = ml_dtypes.bfloat16


def bf(x):
    return np.asarray(x, np.float32).astype(BF16)


def f32(x):
    return np.asarray(x, np.float32)


def f64(x):
    return np.asarray(x).astype(np.float64)


def striped(idx):
    return np.tile(idx.reshape(-1, 16).T, (8, 1))


C, H, S, N = 128, 256, 1024, 128


def setup_inputs():
    return {
        "base": f32(0.1 * np.random.standard_normal((C, S))),
        "z1": f32(np.random.standard_normal((H, N))),
        "w2": bf(1.5 * np.random.standard_normal((H, H)) / np.sqrt(H)),
        "b2": f32(0.3 * np.random.standard_normal((H, 1))),
        "w3": bf(3.0 * np.random.standard_normal((H, C)) / np.sqrt(H)),
        "b3": f32(0.5 * np.random.standard_normal((C, 1))),
        "offs": striped(np.random.permutation(S)[:N]),
    }


def reference(base, z1, w2, b2, w3, b3, offs):
    idx = offs[:16].T.reshape(-1)
    h1 = np.tanh(f64(z1))
    h2 = np.tanh(f64(w2).T @ h1 + f64(b2))
    e = np.exp(f64(w3).T @ h2 + f64(b3))
    r = 1.0 / e.sum(axis=0, keepdims=True)
    out = f64(base).copy()
    out[:, idx] = e * r
    return out

@@ -1,0 +1,82 @@
+import concourse.mybir as mybir
+from concourse.masks import make_identity
+
+F32, BF16, U16 = mybir.dt.float32, mybir.dt.bfloat16, mybir.dt.uint16
+TANH = mybir.ActivationFunctionType.Tanh
+EXP = mybir.ActivationFunctionType.Exp
+COPY = mybir.ActivationFunctionType.Copy
+
+P = 128
+C, H, S, N = 128, 256, 1024, 128
+HB = H // P
+
+FLOPS = 2 * H * H * N + 2 * H * C * N
+
+
+def tile_ppostructuredinsertionmodel_s_kernel(tc, base, z1, w2, b2, w3, b3, offs, out):
+    nc = tc.nc
+    with (
+        tc.tile_pool(name="held", bufs=1) as held,
+        tc.psum_pool(name="banks", bufs=1) as banks,
+    ):
+        z1_in = [held.tile([P, N], F32, name=f"z1_in{kb}") for kb in range(HB)]
+        for kb in range(HB):
+            nc.sync.dma_start(z1_in[kb][:], z1[kb * P : (kb + 1) * P, :])
+        offsets = held.tile([P, N // 16], U16, name="offsets")
+        nc.sync.dma_start(offsets[:], offs)
+        b2_row = held.tile([1, H], F32, name="b2_row")
+        nc.sync.dma_start(b2_row[:], b2.rearrange("h one -> one h"))
+        b3_row = held.tile([1, C], F32, name="b3_row")
+        nc.sync.dma_start(b3_row[:], b3.rearrange("c one -> one c"))
+        w2_sb = held.tile([P, HB, H], BF16, name="w2_sb")
+        nc.scalar.dma_start(w2_sb[:], w2.rearrange("(kb p) m -> p kb m", p=P))
+        w3_sb = held.tile([P, HB, C], BF16, name="w3_sb")
+        nc.scalar.dma_start(w3_sb[:], w3.rearrange("(mb p) c -> p mb c", p=P))
+        window = held.tile([P, S], F32, name="window")
+        nc.gpsimd.dma_start(window[:], base)
+
+        ones_row = held.tile([1, P], F32, name="ones_row")
+        nc.vector.memset(ones_row[:], 1.0)
+        identity = held.tile([P, P], F32, name="identity")
+        make_identity(nc, identity[:])
+
+        z2 = [banks.tile([P, N], F32, name=f"z2_{mb}") for mb in range(HB)]
+        for mb in range(HB):
+            nc.tensor.matmul(z2[mb][:], b2_row[:, mb * P : (mb + 1) * P], ones_row[:, 0:N], start=True, stop=False)
+        logits = banks.tile([N, C], F32, name="logits")
+        nc.tensor.matmul(logits[:], ones_row[:, 0:N], b3_row[:], start=True, stop=False)
+
+        h1 = [held.tile([P, N], BF16, name=f"h1_{kb}") for kb in range(HB)]
+        for kb in range(HB):
+            nc.scalar.activation(h1[kb][:], z1_in[kb][:], TANH)
+
+        h2 = [held.tile([P, N], BF16, name=f"h2_{mb}") for mb in range(HB)]
+        for mb in range(HB):
+            for kb in range(HB):
+                nc.tensor.matmul(
+                    z2[mb][:], w2_sb[:, kb, mb * P : (mb + 1) * P], h1[kb][:], start=False, stop=(kb == HB - 1)
+                )
+            nc.scalar.activation(h2[mb][:], z2[mb][:], TANH)
+
+        for mb in range(HB):
+            nc.tensor.matmul(logits[:], h2[mb][:], w3_sb[:, mb, :], start=False, stop=(mb == HB - 1))
+
+        neg_max = held.tile([N, 1], F32, name="neg_max")
+        nc.vector.reduce_max(neg_max[:], logits[:], axis=mybir.AxisListType.X, negate=True)
+        e_by_sample = held.tile([N, C], F32, name="e_by_sample")
+        e_sum = held.tile([N, 1], F32, name="e_sum")
+        nc.scalar.activation(e_by_sample[:], logits[:], EXP, bias=neg_max[:], accum_out=e_sum[:])
+        r = held.tile([N, 1], F32, name="r")
+        nc.vector.reciprocal(r[:], e_sum[:])
+
+        e_bank = banks.tile([C, N], F32, name="e_bank")
+        nc.tensor.transpose(e_bank[:], e_by_sample[:], identity[:])
+        r_bank = banks.tile([C, N], F32, name="r_bank")
+        nc.tensor.transpose(r_bank[:], r[:].to_broadcast([N, C]), identity[:])
+        e = held.tile([C, N], F32, name="e")
+        nc.scalar.activation(e[:], e_bank[:], COPY)
+        r_all = held.tile([C, N], F32, name="r_all")
+        nc.vector.tensor_copy(r_all[:], r_bank[:])
+
+        nc.vector.tensor_tensor(window[:].indirect(offsets[:]), e[:], r_all[:], mybir.AluOpType.mult)
+        nc.sync.dma_start(out, window[:])

@@ -22,12 +22,13 @@ def tile_ppostructuredinsertionmodel_s_kernel(tc, base, z1, w2, b2, w3, b3, offs
         z1_in = [held.tile([P, N], F32, name=f"z1_in{kb}") for kb in range(HB)]
         for kb in range(HB):
             nc.sync.dma_start(z1_in[kb][:], z1[kb * P : (kb + 1) * P, :])
-        offsets = held.tile([P, N // 16], U16, name="offsets")
-        nc.sync.dma_start(offsets[:], offs)
-        b2_row = held.tile([1, H], F32, name="b2_row")
-        nc.sync.dma_start(b2_row[:], b2.rearrange("h one -> one h"))
+        b2_col = [held.tile([P, 1], F32, name=f"b2_col{mb}") for mb in range(HB)]
+        for mb in range(HB):
+            nc.sync.dma_start(b2_col[mb][:], b2[mb * P : (mb + 1) * P, :])
         b3_row = held.tile([1, C], F32, name="b3_row")
         nc.sync.dma_start(b3_row[:], b3.rearrange("c one -> one c"))
+        offsets = held.tile([P, N // 16], U16, name="offsets")
+        nc.sync.dma_start(offsets[:], offs)
         w2_sb = held.tile([P, HB, H], BF16, name="w2_sb")
         nc.scalar.dma_start(w2_sb[:], w2.rearrange("(kb p) m -> p kb m", p=P))
         w3_sb = held.tile([P, HB, C], BF16, name="w3_sb")
@@ -40,24 +41,22 @@ def tile_ppostructuredinsertionmodel_s_kernel(tc, base, z1, w2, b2, w3, b3, offs
         identity = held.tile([P, P], F32, name="identity")
         make_identity(nc, identity[:])
 
-        z2 = [banks.tile([P, N], F32, name=f"z2_{mb}") for mb in range(HB)]
-        for mb in range(HB):
-            nc.tensor.matmul(z2[mb][:], b2_row[:, mb * P : (mb + 1) * P], ones_row[:, 0:N], start=True, stop=False)
-        logits = banks.tile([N, C], F32, name="logits")
-        nc.tensor.matmul(logits[:], ones_row[:, 0:N], b3_row[:], start=True, stop=False)
-
         h1 = [held.tile([P, N], BF16, name=f"h1_{kb}") for kb in range(HB)]
         for kb in range(HB):
             nc.scalar.activation(h1[kb][:], z1_in[kb][:], TANH)
 
+        z2 = [banks.tile([P, N], F32, name=f"z2_{mb}") for mb in range(HB)]
+        for kb in range(HB):
+            for mb in range(HB):
+                nc.tensor.matmul(
+                    z2[mb][:], w2_sb[:, kb, mb * P : (mb + 1) * P], h1[kb][:], start=(kb == 0), stop=(kb == HB - 1)
+                )
         h2 = [held.tile([P, N], BF16, name=f"h2_{mb}") for mb in range(HB)]
         for mb in range(HB):
-            for kb in range(HB):
-                nc.tensor.matmul(
-                    z2[mb][:], w2_sb[:, kb, mb * P : (mb + 1) * P], h1[kb][:], start=False, stop=(kb == HB - 1)
-                )
-            nc.scalar.activation(h2[mb][:], z2[mb][:], TANH)
+            nc.scalar.activation(h2[mb][:], z2[mb][:], TANH, bias=b2_col[mb][:])
 
+        logits = banks.tile([N, C], F32, name="logits")
+        nc.tensor.matmul(logits[:], ones_row[:, 0:N], b3_row[:], start=True, stop=False)
         for mb in range(HB):
             nc.tensor.matmul(logits[:], h2[mb][:], w3_sb[:, mb, :], start=False, stop=(mb == HB - 1))
 

@@ -19,31 +19,31 @@ def tile_ppostructuredinsertionmodel_s_kernel(tc, base, z1, w2, b2, w3, b3, offs
         tc.tile_pool(name="held", bufs=1) as held,
         tc.psum_pool(name="banks", bufs=1) as banks,
     ):
-        z1_in = [held.tile([P, N], F32, name=f"z1_in{kb}") for kb in range(HB)]
-        for kb in range(HB):
-            nc.sync.dma_start(z1_in[kb][:], z1[kb * P : (kb + 1) * P, :])
-        b2_col = [held.tile([P, 1], F32, name=f"b2_col{mb}") for mb in range(HB)]
-        for mb in range(HB):
-            nc.sync.dma_start(b2_col[mb][:], b2[mb * P : (mb + 1) * P, :])
+        z1_in = held.tile([P, HB, N], F32, name="z1_in")
+        nc.sync.dma_start(z1_in[:], z1.rearrange("(kb p) j -> p kb j", p=P))
+        w2_sb = held.tile([P, HB, H], BF16, name="w2_sb")
+        nc.scalar.dma_start(w2_sb[:], w2.rearrange("(kb p) m -> p kb m", p=P))
+        w3_sb = held.tile([P, HB, C], BF16, name="w3_sb")
+        nc.gpsimd.dma_start(w3_sb[:], w3.rearrange("(mb p) c -> p mb c", p=P))
+        b2_col = held.tile([P, HB], F32, name="b2_col")
+        with nc.allow_non_contiguous_dma(reason="256 single elements: b2 goes one element to a partition"):
+            nc.sync.dma_start(b2_col[:], b2.rearrange("(mb p) one -> p (mb one)", p=P))
         b3_row = held.tile([1, C], F32, name="b3_row")
         nc.sync.dma_start(b3_row[:], b3.rearrange("c one -> one c"))
         offsets = held.tile([P, N // 16], U16, name="offsets")
         nc.sync.dma_start(offsets[:], offs)
-        w2_sb = held.tile([P, HB, H], BF16, name="w2_sb")
-        nc.scalar.dma_start(w2_sb[:], w2.rearrange("(kb p) m -> p kb m", p=P))
-        w3_sb = held.tile([P, HB, C], BF16, name="w3_sb")
-        nc.scalar.dma_start(w3_sb[:], w3.rearrange("(mb p) c -> p mb c", p=P))
         window = held.tile([P, S], F32, name="window")
         nc.gpsimd.dma_start(window[:], base)
 
         ones_row = held.tile([1, P], F32, name="ones_row")
         nc.vector.memset(ones_row[:], 1.0)
         identity = held.tile([P, P], F32, name="identity")
-        make_identity(nc, identity[:])
+        nc.vector.memset(identity[:], 0.0)
+        make_identity(nc, identity[:], nomemset=True)
 
         h1 = [held.tile([P, N], BF16, name=f"h1_{kb}") for kb in range(HB)]
         for kb in range(HB):
-            nc.scalar.activation(h1[kb][:], z1_in[kb][:], TANH)
+            nc.scalar.activation(h1[kb][:], z1_in[:, kb, :], TANH)
 
         z2 = [banks.tile([P, N], F32, name=f"z2_{mb}") for mb in range(HB)]
         for kb in range(HB):
@@ -53,7 +53,7 @@ def tile_ppostructuredinsertionmodel_s_kernel(tc, base, z1, w2, b2, w3, b3, offs
                 )
         h2 = [held.tile([P, N], BF16, name=f"h2_{mb}") for mb in range(HB)]
         for mb in range(HB):
-            nc.scalar.activation(h2[mb][:], z2[mb][:], TANH, bias=b2_col[mb][:])
+            nc.scalar.activation(h2[mb][:], z2[mb][:], TANH, bias=b2_col[:, mb : mb + 1])
 
         logits = banks.tile([N, C], F32, name="logits")
         nc.tensor.matmul(logits[:], ones_row[:, 0:N], b3_row[:], start=True, stop=False)

@@ -9,6 +9,7 @@ COPY = mybir.ActivationFunctionType.Copy
 P = 128
 C, H, S, N = 128, 256, 1024, 128
 HB = H // P
+OFFSETS_PER_COLUMN = 16
 
 FLOPS = 2 * H * H * N + 2 * H * C * N
 
@@ -19,31 +20,31 @@ def tile_ppostructuredinsertionmodel_s_kernel(tc, base, z1, w2, b2, w3, b3, offs
         tc.tile_pool(name="held", bufs=1) as held,
         tc.psum_pool(name="banks", bufs=1) as banks,
     ):
-        z1_in = held.tile([P, HB, N], F32, name="z1_in")
-        nc.sync.dma_start(z1_in[:], z1.rearrange("(kb p) j -> p kb j", p=P))
+        z1_in = [held.tile([P, N], F32, name=f"z1_in{kb}") for kb in range(HB)]
+        for kb in range(HB):
+            nc.sync.dma_start(z1_in[kb][:], z1[kb * P : (kb + 1) * P, :])
         w2_sb = held.tile([P, HB, H], BF16, name="w2_sb")
         nc.scalar.dma_start(w2_sb[:], w2.rearrange("(kb p) m -> p kb m", p=P))
-        w3_sb = held.tile([P, HB, C], BF16, name="w3_sb")
-        nc.gpsimd.dma_start(w3_sb[:], w3.rearrange("(mb p) c -> p mb c", p=P))
-        b2_col = held.tile([P, HB], F32, name="b2_col")
-        with nc.allow_non_contiguous_dma(reason="256 single elements: b2 goes one element to a partition"):
-            nc.sync.dma_start(b2_col[:], b2.rearrange("(mb p) one -> p (mb one)", p=P))
-        b3_row = held.tile([1, C], F32, name="b3_row")
-        nc.sync.dma_start(b3_row[:], b3.rearrange("c one -> one c"))
-        offsets = held.tile([P, N // 16], U16, name="offsets")
-        nc.sync.dma_start(offsets[:], offs)
         window = held.tile([P, S], F32, name="window")
         nc.gpsimd.dma_start(window[:], base)
+        b2_col = held.tile([P, HB], F32, name="b2_col")
+        with nc.allow_non_contiguous_dma(reason="b2 goes one element to a partition: 256 single elements"):
+            nc.sync.dma_start(b2_col[:], b2.rearrange("(mb p) one -> p (mb one)", p=P))
+        w3_sb = held.tile([P, HB, C], BF16, name="w3_sb")
+        nc.sync.dma_start(w3_sb[:], w3.rearrange("(mb p) c -> p mb c", p=P))
+        b3_row = held.tile([1, C], F32, name="b3_row")
+        nc.sync.dma_start(b3_row[:], b3.rearrange("c one -> one c"))
+        offsets = held.tile([P, N // OFFSETS_PER_COLUMN], U16, name="offsets")
+        nc.sync.dma_start(offsets[:], offs)
 
-        ones_row = held.tile([1, P], F32, name="ones_row")
+        ones_row = held.tile([1, N], F32, name="ones_row")
         nc.vector.memset(ones_row[:], 1.0)
         identity = held.tile([P, P], F32, name="identity")
-        nc.vector.memset(identity[:], 0.0)
-        make_identity(nc, identity[:], nomemset=True)
+        make_identity(nc, identity[:])
 
         h1 = [held.tile([P, N], BF16, name=f"h1_{kb}") for kb in range(HB)]
         for kb in range(HB):
-            nc.scalar.activation(h1[kb][:], z1_in[:, kb, :], TANH)
+            nc.scalar.activation(h1[kb][:], z1_in[kb][:], TANH)
 
         z2 = [banks.tile([P, N], F32, name=f"z2_{mb}") for mb in range(HB)]
         for kb in range(HB):
@@ -56,7 +57,7 @@ def tile_ppostructuredinsertionmodel_s_kernel(tc, base, z1, w2, b2, w3, b3, offs
             nc.scalar.activation(h2[mb][:], z2[mb][:], TANH, bias=b2_col[:, mb : mb + 1])
 
         logits = banks.tile([N, C], F32, name="logits")
-        nc.tensor.matmul(logits[:], ones_row[:, 0:N], b3_row[:], start=True, stop=False)
+        nc.tensor.matmul(logits[:], ones_row[:], b3_row[:], start=True, stop=False)
         for mb in range(HB):
             nc.tensor.matmul(logits[:], h2[mb][:], w3_sb[:, mb, :], start=False, stop=(mb == HB - 1))
 

@@ -25,17 +25,17 @@ def tile_ppostructuredinsertionmodel_s_kernel(tc, base, z1, w2, b2, w3, b3, offs
             nc.sync.dma_start(z1_in[kb][:], z1[kb * P : (kb + 1) * P, :])
         w2_sb = held.tile([P, HB, H], BF16, name="w2_sb")
         nc.scalar.dma_start(w2_sb[:], w2.rearrange("(kb p) m -> p kb m", p=P))
-        window = held.tile([P, S], F32, name="window")
-        nc.gpsimd.dma_start(window[:], base)
-        b2_col = held.tile([P, HB], F32, name="b2_col")
-        with nc.allow_non_contiguous_dma(reason="b2 goes one element to a partition: 256 single elements"):
-            nc.sync.dma_start(b2_col[:], b2.rearrange("(mb p) one -> p (mb one)", p=P))
         w3_sb = held.tile([P, HB, C], BF16, name="w3_sb")
-        nc.sync.dma_start(w3_sb[:], w3.rearrange("(mb p) c -> p mb c", p=P))
+        nc.scalar.dma_start(w3_sb[:], w3.rearrange("(mb p) c -> p mb c", p=P))
         b3_row = held.tile([1, C], F32, name="b3_row")
         nc.sync.dma_start(b3_row[:], b3.rearrange("c one -> one c"))
+        b2_col = [held.tile([P, 1], F32, name=f"b2_col{mb}") for mb in range(HB)]
+        for mb in range(HB):
+            nc.sync.dma_start(b2_col[mb][:], b2[mb * P : (mb + 1) * P, :])
         offsets = held.tile([P, N // OFFSETS_PER_COLUMN], U16, name="offsets")
         nc.sync.dma_start(offsets[:], offs)
+        window = held.tile([P, S], F32, name="window")
+        nc.sync.dma_start(window[:], base)
 
         ones_row = held.tile([1, N], F32, name="ones_row")
         nc.vector.memset(ones_row[:], 1.0)
@@ -54,7 +54,7 @@ def tile_ppostructuredinsertionmodel_s_kernel(tc, base, z1, w2, b2, w3, b3, offs
                 )
         h2 = [held.tile([P, N], BF16, name=f"h2_{mb}") for mb in range(HB)]
         for mb in range(HB):
-            nc.scalar.activation(h2[mb][:], z2[mb][:], TANH, bias=b2_col[:, mb : mb + 1])
+            nc.scalar.activation(h2[mb][:], z2[mb][:], TANH, bias=b2_col[mb][:])
 
         logits = banks.tile([N, C], F32, name="logits")
         nc.tensor.matmul(logits[:], ones_row[:], b3_row[:], start=True, stop=False)

@@ -25,17 +25,17 @@ def tile_ppostructuredinsertionmodel_s_kernel(tc, base, z1, w2, b2, w3, b3, offs
             nc.sync.dma_start(z1_in[kb][:], z1[kb * P : (kb + 1) * P, :])
         w2_sb = held.tile([P, HB, H], BF16, name="w2_sb")
         nc.scalar.dma_start(w2_sb[:], w2.rearrange("(kb p) m -> p kb m", p=P))
+        window = held.tile([P, S], F32, name="window")
+        nc.gpsimd.dma_start(window[:], base)
+        b2_col = held.tile([P, HB], F32, name="b2_col")
+        with nc.allow_non_contiguous_dma(reason="b2 goes one element to a partition: 256 single elements"):
+            nc.scalar.dma_start(b2_col[:], b2.rearrange("(mb p) one -> p (mb one)", p=P))
         w3_sb = held.tile([P, HB, C], BF16, name="w3_sb")
-        nc.scalar.dma_start(w3_sb[:], w3.rearrange("(mb p) c -> p mb c", p=P))
-        b3_row = held.tile([1, C], F32, name="b3_row")
-        nc.sync.dma_start(b3_row[:], b3.rearrange("c one -> one c"))
-        b2_col = [held.tile([P, 1], F32, name=f"b2_col{mb}") for mb in range(HB)]
-        for mb in range(HB):
-            nc.sync.dma_start(b2_col[mb][:], b2[mb * P : (mb + 1) * P, :])
+        nc.sync.dma_start(w3_sb[:], w3.rearrange("(mb p) c -> p mb c", p=P))
         offsets = held.tile([P, N // OFFSETS_PER_COLUMN], U16, name="offsets")
         nc.sync.dma_start(offsets[:], offs)
-        window = held.tile([P, S], F32, name="window")
-        nc.sync.dma_start(window[:], base)
+        b3_row = held.tile([1, C], F32, name="b3_row")
+        nc.sync.dma_start(b3_row[:], b3.rearrange("c one -> one c"))
 
         ones_row = held.tile([1, N], F32, name="ones_row")
         nc.vector.memset(ones_row[:], 1.0)
@@ -54,7 +54,7 @@ def tile_ppostructuredinsertionmodel_s_kernel(tc, base, z1, w2, b2, w3, b3, offs
                 )
         h2 = [held.tile([P, N], BF16, name=f"h2_{mb}") for mb in range(HB)]
         for mb in range(HB):
-            nc.scalar.activation(h2[mb][:], z2[mb][:], TANH, bias=b2_col[mb][:])
+            nc.scalar.activation(h2[mb][:], z2[mb][:], TANH, bias=b2_col[:, mb : mb + 1])
 
         logits = banks.tile([N, C], F32, name="logits")
         nc.tensor.matmul(logits[:], ones_row[:], b3_row[:], start=True, stop=False)

@@ -4,7 +4,6 @@ from concourse.masks import make_identity
 F32, BF16, U16 = mybir.dt.float32, mybir.dt.bfloat16, mybir.dt.uint16
 TANH = mybir.ActivationFunctionType.Tanh
 EXP = mybir.ActivationFunctionType.Exp
-COPY = mybir.ActivationFunctionType.Copy
 
 P = 128
 C, H, S, N = 128, 256, 1024, 128
@@ -74,7 +73,7 @@ def tile_ppostructuredinsertionmodel_s_kernel(tc, base, z1, w2, b2, w3, b3, offs
         r_bank = banks.tile([C, N], F32, name="r_bank")
         nc.tensor.transpose(r_bank[:], r[:].to_broadcast([N, C]), identity[:])
         e = held.tile([C, N], F32, name="e")
-        nc.scalar.activation(e[:], e_bank[:], COPY)
+        nc.vector.tensor_copy(e[:], e_bank[:])
         r_all = held.tile([C, N], F32, name="r_all")
         nc.vector.tensor_copy(r_all[:], r_bank[:])
 

@@ -60,11 +60,9 @@ def tile_ppostructuredinsertionmodel_s_kernel(tc, base, z1, w2, b2, w3, b3, offs
         for mb in range(HB):
             nc.tensor.matmul(logits[:], h2[mb][:], w3_sb[:, mb, :], start=False, stop=(mb == HB - 1))
 
-        neg_max = held.tile([N, 1], F32, name="neg_max")
-        nc.vector.reduce_max(neg_max[:], logits[:], axis=mybir.AxisListType.X, negate=True)
         e_by_sample = held.tile([N, C], F32, name="e_by_sample")
         e_sum = held.tile([N, 1], F32, name="e_sum")
-        nc.scalar.activation(e_by_sample[:], logits[:], EXP, bias=neg_max[:], accum_out=e_sum[:])
+        nc.scalar.activation(e_by_sample[:], logits[:], EXP, accum_out=e_sum[:])
         r = held.tile([N, 1], F32, name="r")
         nc.vector.reciprocal(r[:], e_sum[:])
 

@@ -21,9 +21,9 @@ def tile_ppostructuredinsertionmodel_s_kernel(tc, base, z1, w2, b2, w3, b3, offs
     ):
         z1_in = [held.tile([P, N], F32, name=f"z1_in{kb}") for kb in range(HB)]
         for kb in range(HB):
-            nc.sync.dma_start(z1_in[kb][:], z1[kb * P : (kb + 1) * P, :])
+            nc.sync.dma_start(z1_in[kb][:], z1.rearrange("(p kb) n -> p kb n", kb=HB)[:, kb, :])
         w2_sb = held.tile([P, HB, H], BF16, name="w2_sb")
-        nc.scalar.dma_start(w2_sb[:], w2.rearrange("(kb p) m -> p kb m", p=P))
+        nc.scalar.dma_start(w2_sb[:], w2.rearrange("(p kb) m -> p kb m", kb=HB))
         window = held.tile([P, S], F32, name="window")
         nc.gpsimd.dma_start(window[:], base)
         b2_col = held.tile([P, HB], F32, name="b2_col")

@@ -19,16 +19,15 @@ def tile_ppostructuredinsertionmodel_s_kernel(tc, base, z1, w2, b2, w3, b3, offs
         tc.tile_pool(name="held", bufs=1) as held,
         tc.psum_pool(name="banks", bufs=1) as banks,
     ):
-        z1_in = [held.tile([P, N], F32, name=f"z1_in{kb}") for kb in range(HB)]
-        for kb in range(HB):
-            nc.sync.dma_start(z1_in[kb][:], z1.rearrange("(p kb) n -> p kb n", kb=HB)[:, kb, :])
+        z1_in = held.tile([P, HB, N], F32, name="z1_in")
+        nc.sync.dma_start(z1_in[:], z1.rearrange("(p kb) n -> p kb n", kb=HB))
         w2_sb = held.tile([P, HB, H], BF16, name="w2_sb")
         nc.scalar.dma_start(w2_sb[:], w2.rearrange("(p kb) m -> p kb m", kb=HB))
         window = held.tile([P, S], F32, name="window")
         nc.gpsimd.dma_start(window[:], base)
         b2_col = held.tile([P, HB], F32, name="b2_col")
         with nc.allow_non_contiguous_dma(reason="b2 goes one element to a partition: 256 single elements"):
-            nc.scalar.dma_start(b2_col[:], b2.rearrange("(mb p) one -> p (mb one)", p=P))
+            nc.sync.dma_start(b2_col[:], b2.rearrange("(mb p) one -> p (mb one)", p=P))
         w3_sb = held.tile([P, HB, C], BF16, name="w3_sb")
         nc.sync.dma_start(w3_sb[:], w3.rearrange("(mb p) c -> p mb c", p=P))
         offsets = held.tile([P, N // OFFSETS_PER_COLUMN], U16, name="offsets")
@@ -43,7 +42,7 @@ def tile_ppostructuredinsertionmodel_s_kernel(tc, base, z1, w2, b2, w3, b3, offs
 
         h1 = [held.tile([P, N], BF16, name=f"h1_{kb}") for kb in range(HB)]
         for kb in range(HB):
-            nc.scalar.activation(h1[kb][:], z1_in[kb][:], TANH)
+            nc.scalar.activation(h1[kb][:], z1_in[:, kb, :], TANH)
 
         z2 = [banks.tile([P, N], F32, name=f"z2_{mb}") for mb in range(HB)]
         for kb in range(HB):

@@ -23,8 +23,6 @@ def tile_ppostructuredinsertionmodel_s_kernel(tc, base, z1, w2, b2, w3, b3, offs
         nc.sync.dma_start(z1_in[:], z1.rearrange("(p kb) n -> p kb n", kb=HB))
         w2_sb = held.tile([P, HB, H], BF16, name="w2_sb")
         nc.scalar.dma_start(w2_sb[:], w2.rearrange("(p kb) m -> p kb m", kb=HB))
-        window = held.tile([P, S], F32, name="window")
-        nc.gpsimd.dma_start(window[:], base)
         b2_col = held.tile([P, HB], F32, name="b2_col")
         with nc.allow_non_contiguous_dma(reason="b2 goes one element to a partition: 256 single elements"):
             nc.sync.dma_start(b2_col[:], b2.rearrange("(mb p) one -> p (mb one)", p=P))
@@ -32,13 +30,13 @@ def tile_ppostructuredinsertionmodel_s_kernel(tc, base, z1, w2, b2, w3, b3, offs
         nc.sync.dma_start(w3_sb[:], w3.rearrange("(mb p) c -> p mb c", p=P))
         offsets = held.tile([P, N // OFFSETS_PER_COLUMN], U16, name="offsets")
         nc.sync.dma_start(offsets[:], offs)
-        b3_row = held.tile([1, C], F32, name="b3_row")
-        nc.sync.dma_start(b3_row[:], b3.rearrange("c one -> one c"))
+        b3_col = held.tile([C, 1], F32, name="b3_col")
+        nc.sync.dma_start(b3_col[:], b3)
 
-        ones_row = held.tile([1, N], F32, name="ones_row")
-        nc.vector.memset(ones_row[:], 1.0)
         identity = held.tile([P, P], F32, name="identity")
         make_identity(nc, identity[:])
+        window = held.tile([P, S], F32, name="window")
+        nc.gpsimd.dma_start(window[:], base)
 
         h1 = [held.tile([P, N], BF16, name=f"h1_{kb}") for kb in range(HB)]
         for kb in range(HB):
@@ -55,7 +53,9 @@ def tile_ppostructuredinsertionmodel_s_kernel(tc, base, z1, w2, b2, w3, b3, offs
             nc.scalar.activation(h2[mb][:], z2[mb][:], TANH, bias=b2_col[:, mb : mb + 1])
 
         logits = banks.tile([N, C], F32, name="logits")
-        nc.tensor.matmul(logits[:], ones_row[:], b3_row[:], start=True, stop=False)
+        nc.tensor.matmul(
+            logits[:], b3_col[:].to_broadcast([C, N]), identity[:], is_transpose=True, start=True, stop=False
+        )
         for mb in range(HB):
             nc.tensor.matmul(logits[:], h2[mb][:], w3_sb[:, mb, :], start=False, stop=(mb == HB - 1))
 

@@ -23,6 +23,8 @@ def tile_ppostructuredinsertionmodel_s_kernel(tc, base, z1, w2, b2, w3, b3, offs
         nc.sync.dma_start(z1_in[:], z1.rearrange("(p kb) n -> p kb n", kb=HB))
         w2_sb = held.tile([P, HB, H], BF16, name="w2_sb")
         nc.scalar.dma_start(w2_sb[:], w2.rearrange("(p kb) m -> p kb m", kb=HB))
+        b3_col = held.tile([C, 1], F32, name="b3_col")
+        nc.sync.dma_start(b3_col[:], b3)
         b2_col = held.tile([P, HB], F32, name="b2_col")
         with nc.allow_non_contiguous_dma(reason="b2 goes one element to a partition: 256 single elements"):
             nc.sync.dma_start(b2_col[:], b2.rearrange("(mb p) one -> p (mb one)", p=P))
@@ -30,13 +32,16 @@ def tile_ppostructuredinsertionmodel_s_kernel(tc, base, z1, w2, b2, w3, b3, offs
         nc.sync.dma_start(w3_sb[:], w3.rearrange("(mb p) c -> p mb c", p=P))
         offsets = held.tile([P, N // OFFSETS_PER_COLUMN], U16, name="offsets")
         nc.sync.dma_start(offsets[:], offs)
-        b3_col = held.tile([C, 1], F32, name="b3_col")
-        nc.sync.dma_start(b3_col[:], b3)
 
         identity = held.tile([P, P], F32, name="identity")
         make_identity(nc, identity[:])
         window = held.tile([P, S], F32, name="window")
         nc.gpsimd.dma_start(window[:], base)
+
+        logits = banks.tile([N, C], F32, name="logits")
+        nc.tensor.matmul(
+            logits[:], b3_col[:].to_broadcast([C, N]), identity[:], is_transpose=True, start=True, stop=False
+        )
 
         h1 = [held.tile([P, N], BF16, name=f"h1_{kb}") for kb in range(HB)]
         for kb in range(HB):
@@ -52,10 +57,6 @@ def tile_ppostructuredinsertionmodel_s_kernel(tc, base, z1, w2, b2, w3, b3, offs
         for mb in range(HB):
             nc.scalar.activation(h2[mb][:], z2[mb][:], TANH, bias=b2_col[:, mb : mb + 1])
 
-        logits = banks.tile([N, C], F32, name="logits")
-        nc.tensor.matmul(
-            logits[:], b3_col[:].to_broadcast([C, N]), identity[:], is_transpose=True, start=True, stop=False
-        )
         for mb in range(HB):
             nc.tensor.matmul(logits[:], h2[mb][:], w3_sb[:, mb, :], start=False, stop=(mb == HB - 1))
 

@@ -21,15 +21,14 @@ def tile_ppostructuredinsertionmodel_s_kernel(tc, base, z1, w2, b2, w3, b3, offs
     ):
         z1_in = held.tile([P, HB, N], F32, name="z1_in")
         nc.sync.dma_start(z1_in[:], z1.rearrange("(p kb) n -> p kb n", kb=HB))
-        w2_sb = held.tile([P, HB, H], BF16, name="w2_sb")
-        nc.scalar.dma_start(w2_sb[:], w2.rearrange("(p kb) m -> p kb m", kb=HB))
+        w2_sb = held.tile([P, HB, P, HB], BF16, name="w2_sb")
+        nc.scalar.dma_start(w2_sb[:], w2.rearrange("(p kb) (q mb) -> p kb q mb", kb=HB, mb=HB))
         b3_col = held.tile([C, 1], F32, name="b3_col")
         nc.sync.dma_start(b3_col[:], b3)
         b2_col = held.tile([P, HB], F32, name="b2_col")
-        with nc.allow_non_contiguous_dma(reason="b2 goes one element to a partition: 256 single elements"):
-            nc.sync.dma_start(b2_col[:], b2.rearrange("(mb p) one -> p (mb one)", p=P))
+        nc.sync.dma_start(b2_col[:], b2.rearrange("(q mb) one -> q (mb one)", mb=HB))
         w3_sb = held.tile([P, HB, C], BF16, name="w3_sb")
-        nc.sync.dma_start(w3_sb[:], w3.rearrange("(mb p) c -> p mb c", p=P))
+        nc.sync.dma_start(w3_sb[:], w3.rearrange("(q mb) c -> q mb c", mb=HB))
         offsets = held.tile([P, N // OFFSETS_PER_COLUMN], U16, name="offsets")
         nc.sync.dma_start(offsets[:], offs)
 
@@ -50,9 +49,7 @@ def tile_ppostructuredinsertionmodel_s_kernel(tc, base, z1, w2, b2, w3, b3, offs
         z2 = [banks.tile([P, N], F32, name=f"z2_{mb}") for mb in range(HB)]
         for kb in range(HB):
             for mb in range(HB):
-                nc.tensor.matmul(
-                    z2[mb][:], w2_sb[:, kb, mb * P : (mb + 1) * P], h1[kb][:], start=(kb == 0), stop=(kb == HB - 1)
-                )
+                nc.tensor.matmul(z2[mb][:], w2_sb[:, kb, :, mb], h1[kb][:], start=(kb == 0), stop=(kb == HB - 1))
         h2 = [held.tile([P, N], BF16, name=f"h2_{mb}") for mb in range(HB)]
         for mb in range(HB):
             nc.scalar.activation(h2[mb][:], z2[mb][:], TANH, bias=b2_col[:, mb : mb + 1])

@@ -8,6 +8,7 @@ EXP = mybir.ActivationFunctionType.Exp
 P = 128
 C, H, S, N = 128, 256, 1024, 128
 HB = H // P
+NH = N // 2
 OFFSETS_PER_COLUMN = 16
 
 FLOPS = 2 * H * H * N + 2 * H * C * N
@@ -42,17 +43,21 @@ def tile_ppostructuredinsertionmodel_s_kernel(tc, base, z1, w2, b2, w3, b3, offs
             logits[:], b3_col[:].to_broadcast([C, N]), identity[:], is_transpose=True, start=True, stop=False
         )
 
+        halves = [slice(start, start + NH) for start in range(0, N, NH)]
         h1 = [held.tile([P, N], BF16, name=f"h1_{kb}") for kb in range(HB)]
-        for kb in range(HB):
-            nc.scalar.activation(h1[kb][:], z1_in[:, kb, :], TANH)
-
-        z2 = [banks.tile([P, N], F32, name=f"z2_{mb}") for mb in range(HB)]
-        for kb in range(HB):
-            for mb in range(HB):
-                nc.tensor.matmul(z2[mb][:], w2_sb[:, kb, :, mb], h1[kb][:], start=(kb == 0), stop=(kb == HB - 1))
+        for half in halves:
+            for kb in range(HB):
+                nc.scalar.activation(h1[kb][:, half], z1_in[:, kb, half], TANH)
         h2 = [held.tile([P, N], BF16, name=f"h2_{mb}") for mb in range(HB)]
-        for mb in range(HB):
-            nc.scalar.activation(h2[mb][:], z2[mb][:], TANH, bias=b2_col[:, mb : mb + 1])
+        for half in halves:
+            z2 = [banks.tile([P, NH], F32, name=f"z2_{mb}_{half.start}") for mb in range(HB)]
+            for kb in range(HB):
+                for mb in range(HB):
+                    nc.tensor.matmul(
+                        z2[mb][:], w2_sb[:, kb, :, mb], h1[kb][:, half], start=(kb == 0), stop=(kb == HB - 1)
+                    )
+            for mb in range(HB):
+                nc.scalar.activation(h2[mb][:, half], z2[mb][:], TANH, bias=b2_col[:, mb : mb + 1])
 
         for mb in range(HB):
             nc.tensor.matmul(logits[:], h2[mb][:], w3_sb[:, mb, :], start=False, stop=(mb == HB - 1))

@@ -51,8 +51,8 @@ def tile_ppostructuredinsertionmodel_s_kernel(tc, base, z1, w2, b2, w3, b3, offs
         h2 = [held.tile([P, N], BF16, name=f"h2_{mb}") for mb in range(HB)]
         for half in halves:
             z2 = [banks.tile([P, NH], F32, name=f"z2_{mb}_{half.start}") for mb in range(HB)]
-            for kb in range(HB):
-                for mb in range(HB):
+            for mb in range(HB):
+                for kb in range(HB):
                     nc.tensor.matmul(
                         z2[mb][:], w2_sb[:, kb, :, mb], h1[kb][:, half], start=(kb == 0), stop=(kb == HB - 1)
                     )

import concourse.mybir as mybir
from concourse.masks import make_identity

F32, BF16, U16 = mybir.dt.float32, mybir.dt.bfloat16, mybir.dt.uint16
TANH = mybir.ActivationFunctionType.Tanh
EXP = mybir.ActivationFunctionType.Exp

P = 128
C, H, S, N = 128, 256, 1024, 128
HB = H // P
NH = N // 2
OFFSETS_PER_COLUMN = 16

FLOPS = 2 * H * H * N + 2 * H * C * N


def tile_ppostructuredinsertionmodel_s_kernel(tc, base, z1, w2, b2, w3, b3, offs, out):
    nc = tc.nc
    with (
        tc.tile_pool(name="held", bufs=1) as held,
        tc.psum_pool(name="banks", bufs=1) as banks,
    ):
        z1_in = held.tile([P, HB, N], F32, name="z1_in")
        nc.sync.dma_start(z1_in[:], z1.rearrange("(p kb) n -> p kb n", kb=HB))
        w2_sb = held.tile([P, HB, P, HB], BF16, name="w2_sb")
        nc.scalar.dma_start(w2_sb[:], w2.rearrange("(p kb) (q mb) -> p kb q mb", kb=HB, mb=HB))
        b3_col = held.tile([C, 1], F32, name="b3_col")
        nc.sync.dma_start(b3_col[:], b3)
        b2_col = held.tile([P, HB], F32, name="b2_col")
        nc.sync.dma_start(b2_col[:], b2.rearrange("(q mb) one -> q (mb one)", mb=HB))
        w3_sb = held.tile([P, HB, C], BF16, name="w3_sb")
        nc.sync.dma_start(w3_sb[:], w3.rearrange("(q mb) c -> q mb c", mb=HB))
        offsets = held.tile([P, N // OFFSETS_PER_COLUMN], U16, name="offsets")
        nc.sync.dma_start(offsets[:], offs)

        identity = held.tile([P, P], F32, name="identity")
        make_identity(nc, identity[:])
        window = held.tile([P, S], F32, name="window")
        nc.gpsimd.dma_start(window[:], base)

        logits = banks.tile([N, C], F32, name="logits")
        nc.tensor.matmul(
            logits[:], b3_col[:].to_broadcast([C, N]), identity[:], is_transpose=True, start=True, stop=False
        )

        halves = [slice(start, start + NH) for start in range(0, N, NH)]
        h1 = [held.tile([P, N], BF16, name=f"h1_{kb}") for kb in range(HB)]
        for half in halves:
            for kb in range(HB):
                nc.scalar.activation(h1[kb][:, half], z1_in[:, kb, half], TANH)
        h2 = [held.tile([P, N], BF16, name=f"h2_{mb}") for mb in range(HB)]
        for half in halves:
            z2 = [banks.tile([P, NH], F32, name=f"z2_{mb}_{half.start}") for mb in range(HB)]
            for mb in range(HB):
                for kb in range(HB):
                    nc.tensor.matmul(
                        z2[mb][:], w2_sb[:, kb, :, mb], h1[kb][:, half], start=(kb == 0), stop=(kb == HB - 1)
                    )
            for mb in range(HB):
                nc.scalar.activation(h2[mb][:, half], z2[mb][:], TANH, bias=b2_col[:, mb : mb + 1])

        for mb in range(HB):
            nc.tensor.matmul(logits[:], h2[mb][:], w3_sb[:, mb, :], start=False, stop=(mb == HB - 1))

        e_by_sample = held.tile([N, C], F32, name="e_by_sample")
        e_sum = held.tile([N, 1], F32, name="e_sum")
        nc.scalar.activation(e_by_sample[:], logits[:], EXP, accum_out=e_sum[:])
        r = held.tile([N, 1], F32, name="r")
        nc.vector.reciprocal(r[:], e_sum[:])

        e_bank = banks.tile([C, N], F32, name="e_bank")
        nc.tensor.transpose(e_bank[:], e_by_sample[:], identity[:])
        r_bank = banks.tile([C, N], F32, name="r_bank")
        nc.tensor.transpose(r_bank[:], r[:].to_broadcast([N, C]), identity[:])
        e = held.tile([C, N], F32, name="e")
        nc.vector.tensor_copy(e[:], e_bank[:])
        r_all = held.tile([C, N], F32, name="r_all")
        nc.vector.tensor_copy(r_all[:], r_bank[:])

        nc.vector.tensor_tensor(window[:].indirect(offsets[:]), e[:], r_all[:], mybir.AluOpType.mult)
        nc.sync.dma_start(out, window[:])
